import numpy as np
import ml_dtypes


def mxq(x, axis, fmt="e4m3"):
    dtype, down = {"e4m3": (ml_dtypes.float8_e4m3fn, 7), "e5m2": (ml_dtypes.float8_e5m2, 14)}[fmt]
    v = np.moveaxis(np.asarray(x, np.float32).astype(ml_dtypes.bfloat16).astype(np.float64), axis, -1)
    blocks = v.reshape(v.shape[:-1] + (-1, 32))
    amax = np.abs(blocks).max(-1, keepdims=True)
    byte = np.maximum(np.where(amax > 0, np.frexp(amax)[1] - 1 + 127, 0) - down, 1)
    scale = np.exp2(byte - 127.0)
    codes = (blocks / scale).astype(np.float32).astype(dtype).astype(np.float64)
    return np.moveaxis((codes * scale).reshape(v.shape), -1, axis)


WIDE = False


def mx_kscale(k):
    if not WIDE:
        return np.ones(k)
    levels = np.array([10, -10, 5, -5, 0])
    a = np.random.permutation(np.resize(levels, k // 512 * 4)).reshape(k // 512, 4)
    idx = np.arange(k)
    return np.exp2(a[idx // 512, idx % 128 // 32])


BF16 = ml_dtypes.bfloat16


def bf(x):
    return np.asarray(x, np.float32).astype(BF16)


def f64(x):
    return np.asarray(x).astype(np.float64)


E2M1 = np.array([0.0, 0.5, 1.0, 1.5, 2.0, 3.0, 4.0, 6.0, -0.0, -0.5, -1.0, -1.5, -2.0, -3.0, -4.0, -6.0])


def pack_weight(w, fmt):
    k, n = w.shape
    w = f64(bf(w)).reshape(k // 32, 32, n)
    amax = np.abs(w).max(1)
    if fmt == "e4m3":
        byte = np.frexp(amax)[1] - 1 + 127 - 7
    else:
        mant, ex = np.frexp(amax / 6.0)
        byte = np.where(mant > 0.5, ex, ex - 1) + 127
    byte = np.clip(np.where(amax > 0, byte, 1), 1, 254)
    scaled = (w * np.exp2(127.0 - byte)[:, None, :]).reshape(k, n).astype(np.float32)
    by_word = np.ascontiguousarray(scaled.reshape(k // 512, 128, 4, n).transpose(0, 1, 3, 2))
    if fmt == "e4m3":
        words = by_word.astype(ml_dtypes.float8_e4m3fn).view(np.uint8)
    else:
        c = by_word.astype(ml_dtypes.float4_e2m1fn).view(np.uint8) & 0xF
        words = c[..., 0::2] | (c[..., 1::2] << 4)
    return np.ascontiguousarray(words), np.ascontiguousarray(byte.astype(np.uint8).reshape(k // 512, 16, n))


def unpack_weight(words, scales, fmt):
    g, p, n, _ = words.shape
    if fmt == "e4m3":
        vals = np.ascontiguousarray(words).view(ml_dtypes.float8_e4m3fn).astype(np.float64)
    else:
        nib = np.empty((g, p, n, 4), np.uint8)
        nib[..., 0::2] = words & 0xF
        nib[..., 1::2] = words >> 4
        vals = E2M1[nib]
    vals = vals * np.repeat(np.exp2(scales.astype(np.float64) - 127.0), 8, axis=1)[..., None]
    return vals.transpose(0, 1, 3, 2).reshape(g * 512, n)

def pack4(w):
    words, scales = pack_weight(w, "e2m1")
    return words.reshape(words.shape[0], 128, -1), scales


def unpack4(words, scales):
    return unpack_weight(words.reshape(words.shape[0], 128, -1, 2), scales, "e2m1")


B, T, D, H, KVH, HD = 2, 128, 16384, 16, 4, 128
HALF = HD // 2
EPS = 1e-6
ROPE_BASE = 10000.0


def zc_rmsnorm(x, scale):
    rms = np.sqrt(np.mean(x ** 2, axis=-1, keepdims=True) + EPS)
    return (1.0 + scale) * x / rms


def apply_rope(x, cos, sin):
    t = x.shape[2]
    c = cos[:t][None, None, :, :]
    s = sin[:t][None, None, :, :]
    x1, x2 = x[..., :HALF], x[..., HALF:]
    return np.concatenate([x1 * c - x2 * s, x2 * c + x1 * s], axis=-1)


def setup_inputs():
    s = mx_kscale(D)
    inv_freq = 1.0 / (ROPE_BASE ** (np.arange(0, HALF) / HALF))
    ang = np.arange(T)[:, None] * inv_freq[None, :]
    kv_input = bf(np.random.standard_normal((B, T, D)) * s)
    Wk_words, Wk_scales = pack4(np.random.standard_normal((D, KVH * HD)) / np.sqrt(D) / s[:, None])
    Wv_words, Wv_scales = pack4(np.random.standard_normal((D, KVH * HD)) / np.sqrt(D) / s[:, None])
    return {"kv_input": kv_input,
            "Wk_words": Wk_words, "Wk_scales": Wk_scales,
            "Wv_words": Wv_words, "Wv_scales": Wv_scales,
            "k_scale": bf(np.random.standard_normal(HD) * 0.2),
            "cos": bf(np.cos(ang)), "sin": bf(np.sin(ang))}


def reference(kv_input, Wk_words, Wk_scales, Wv_words, Wv_scales, k_scale, cos, sin):
    b = kv_input.shape[0]
    xq = mxq(f64(kv_input), 2, "e4m3")
    k = (xq @ unpack4(Wk_words, Wk_scales)).reshape(b, -1, KVH, HD).transpose(0, 2, 1, 3)
    v = (xq @ unpack4(Wv_words, Wv_scales)).reshape(b, -1, KVH, HD).transpose(0, 2, 1, 3)
    k = zc_rmsnorm(k, f64(k_scale))
    rep = H // KVH
    k = np.repeat(k, rep, axis=1)
    v = np.repeat(v, rep, axis=1)
    k = apply_rope(k, f64(cos), f64(sin))
    return k, v

@@ -1,0 +1,231 @@
+from contextlib import ExitStack
+
+import concourse.mybir as mybir
+from concourse.masks import make_identity
+
+F32 = mybir.dt.float32
+BF16 = mybir.dt.bfloat16
+I32 = mybir.dt.int32
+U32 = mybir.dt.uint32
+U8 = mybir.dt.uint8
+FP8X4 = mybir.dt.float8_e4m3fn_x4
+FP4X4 = mybir.dt.float4_e2m1fn_x4
+ALU = mybir.AluOpType
+ACT = mybir.ActivationFunctionType
+
+P = 128
+PACK = 4
+K_PASS = P * PACK
+BATCH = 2
+TOKENS = 128
+D_MODEL = 16384
+KV_HEADS = 4
+HEAD_DIM = 128
+HALF = HEAD_DIM // 2
+REPEAT = 4
+N_COLS = KV_HEADS * HEAD_DIM
+EPS = 1e-6
+
+PASSES = D_MODEL // K_PASS
+CHUNK = 4
+CHUNKS = PASSES // CHUNK
+PAIRS = K_PASS // 2
+PREFETCH = 4
+SCALE_ROWS = 4
+
+FLOPS = 2 * BATCH * TOKENS * D_MODEL * 2 * N_COLS
+
+
+def load_scale_rows(nc, planes, scales):
+    for r in range(SCALE_ROWS):
+        nc.sync.dma_start(
+            out=planes[r:P:32, :, :].bitcast(I32),
+            in_=scales[:, r : 4 * SCALE_ROWS : SCALE_ROWS, :].rearrange("g q n -> q g n").bitcast(I32),
+        )
+
+
+def load_weight_words(nc, words_sb, words, c):
+    passes = slice(c * CHUNK, (c + 1) * CHUNK)
+    nc.sync.dma_start(
+        out=words_sb[:, passes, :].bitcast(I32),
+        in_=words[passes].rearrange("g p n -> p g n").bitcast(I32),
+    )
+
+
+def project(nc, acc, x_codes, x_planes, words_sb, planes, c):
+    for b in range(BATCH):
+        for g in range(c * CHUNK, (c + 1) * CHUNK):
+            nc.tensor.matmul_mx(
+                out=acc[b][:].rearrange("p h s c -> p (h s c)"),
+                lhsT=x_codes[:, g, b, :].bitcast(FP8X4),
+                lhsT_scale=x_planes[:, g, b, :],
+                rhs=words_sb[:, g, :].bitcast(FP4X4),
+                rhs_scale=planes[:, g, :],
+                start=(g == 0),
+                stop=(g == PASSES - 1),
+            )
+
+
+def store_heads(nc, out, b, rows):
+    by_repeat = out[b].rearrange("(h r) t d -> r t h d", r=REPEAT)
+    for r in range(REPEAT):
+        nc.sync.dma_start(out=by_repeat[r], in_=rows)
+
+
+def tile_multiheadattention_pb_k_kernel(
+    tc, kv_input, Wk_words, Wk_scales, Wv_words, Wv_scales, k_scale, cos, sin, out_0, out_1
+):
+    nc = tc.nc
+    with ExitStack() as ctx:
+        keep = ctx.enter_context(tc.tile_pool(name="keep", bufs=1))
+        raw_pool = ctx.enter_context(tc.tile_pool(name="raw", bufs=PREFETCH))
+        grouped_pool = ctx.enter_context(tc.tile_pool(name="grouped", bufs=2))
+        work = ctx.enter_context(tc.tile_pool(name="work", bufs=2))
+        banks = ctx.enter_context(tc.psum_pool(name="banks", bufs=4))
+        sums = ctx.enter_context(tc.psum_pool(name="sums", bufs=1))
+        ctx.enter_context(tc.manual_schedule())
+
+        wk_words = keep.tile([P, PASSES, 2 * N_COLS], U8, align_bytes=64)
+        wv_words = keep.tile([P, PASSES, 2 * N_COLS], U8, align_bytes=64)
+        wk_planes = keep.tile([P, PASSES, N_COLS], U8, align_bytes=64)
+        wv_planes = keep.tile([P, PASSES, N_COLS], U8, align_bytes=64)
+        x_codes = keep.tile([P, PASSES, BATCH, TOKENS], U32, align_bytes=64)
+        x_planes = keep.tile([P, PASSES, BATCH, TOKENS], U8, align_bytes=64)
+
+        nc.vector.memset(wk_planes[:].bitcast(I32), 0)
+        nc.vector.memset(wv_planes[:].bitcast(I32), 0)
+
+        identity = keep.tile([P, P], F32)
+        make_identity(nc, identity[:])
+
+        gain_row = keep.tile([P, HEAD_DIM], BF16)
+        ones = keep.tile([P, P], BF16)
+        nc.gpsimd.memset(gain_row[:], 0.0)
+        nc.gpsimd.memset(ones[:], 1.0)
+        nc.scalar.dma_start(out=gain_row[0:1, :], in_=k_scale.unsqueeze(0))
+        cos_sb = keep.tile([P, HALF], BF16)
+        sin_sb = keep.tile([P, HALF], BF16)
+        nc.scalar.dma_start(out=cos_sb[:], in_=cos)
+        nc.scalar.dma_start(out=sin_sb[:], in_=sin)
+
+        raw = {}
+
+        def load_tokens(c):
+            raw[c] = raw_pool.tile([P, BATCH, CHUNK * K_PASS], BF16, name="raw")
+            columns = slice(c * CHUNK * K_PASS, (c + 1) * CHUNK * K_PASS)
+            nc.sync.dma_start(out=raw[c][:], in_=kv_input[:, :, columns].rearrange("b t k -> t b k"))
+
+        load_tokens(0)
+        load_scale_rows(nc, wk_planes, Wk_scales)
+        load_weight_words(nc, wk_words, Wk_words, 0)
+        for c in range(1, PREFETCH):
+            load_tokens(c)
+            load_weight_words(nc, wk_words, Wk_words, c)
+
+        gain_bank = banks.tile([P, 2, HALF], F32, tag="bank")
+        nc.tensor.matmul(
+            out=gain_bank[:].rearrange("p s c -> p (s c)"), lhsT=ones[:], rhs=gain_row[:], start=True, stop=True
+        )
+        gain = keep.tile([P, 2, HALF], F32)
+        cos_gain = keep.tile([P, 2, HALF], F32)
+        sin_gain = keep.tile([P, 2, HALF], F32)
+        nc.vector.tensor_scalar_add(out=gain[:], in0=gain_bank[:], scalar1=1.0)
+        nc.vector.tensor_tensor(
+            out=cos_gain[:], in0=gain[:], in1=cos_sb[:].unsqueeze(1).to_broadcast([P, 2, HALF]), op=ALU.mult
+        )
+        nc.vector.tensor_tensor(
+            out=sin_gain[:], in0=gain[:], in1=sin_sb[:].unsqueeze(1).to_broadcast([P, 2, HALF]), op=ALU.mult
+        )
+        nc.vector.tensor_scalar_mul(out=sin_gain[:, 1, :], in0=sin_gain[:, 1, :], scalar1=-1.0)
+
+        def quantise_chunk(c):
+            pairs = raw[c][:].bitcast(F32)
+            grouped = grouped_pool.tile([P, CHUNK * BATCH, TOKENS, PACK], BF16, align_bytes=64)
+            grouped_pairs = grouped[:].bitcast(F32)
+            for j in range(CHUNK):
+                bank = banks.tile([P, BATCH, 2, TOKENS], F32, tag="bank")
+                for b in range(BATCH):
+                    for u in range(2):
+                        nc.tensor.transpose(
+                            bank[:, b, u, :], pairs[:, b, j * PAIRS + u : (j + 1) * PAIRS : 2], identity[:]
+                        )
+                target = grouped_pairs[:, j * BATCH : (j + 1) * BATCH, :, :]
+                source = bank[:].rearrange("p b u m -> p b m u")
+                if j % 2 == 0:
+                    nc.vector.tensor_copy(out=target, in_=source)
+                else:
+                    nc.scalar.copy(out=target, in_=source)
+            for half in range(2):
+                first = c * CHUNK + half * (CHUNK // 2)
+                passes = slice(first, first + CHUNK // 2)
+                units = slice(half * (CHUNK // 2) * BATCH, (half + 1) * (CHUNK // 2) * BATCH)
+                nc.vector.quantize_mx(
+                    out=x_codes[:, passes, :, :].rearrange("p g b m -> p (g b m)").bitcast(FP8X4),
+                    scales=x_planes[:, passes, :, :].rearrange("p g b m -> p (g b m)"),
+                    in_=grouped[:, units, :, :].rearrange("p a m t -> p (a m t)"),
+                )
+
+        k_sum = [sums.tile([P, KV_HEADS, 2, HALF], F32, name="k_sum%d" % b) for b in range(BATCH)]
+        v_sum = [sums.tile([P, KV_HEADS, 2, HALF], F32, name="v_sum%d" % b) for b in range(BATCH)]
+        for c in range(CHUNKS):
+            quantise_chunk(c)
+            if c + PREFETCH < CHUNKS:
+                load_tokens(c + PREFETCH)
+                load_weight_words(nc, wk_words, Wk_words, c + PREFETCH)
+            if c > 0:
+                project(nc, k_sum, x_codes, x_planes, wk_words, wk_planes, c - 1)
+        project(nc, k_sum, x_codes, x_planes, wk_words, wk_planes, CHUNKS - 1)
+
+        load_scale_rows(nc, wv_planes, Wv_scales)
+        for c in range(CHUNKS):
+            load_weight_words(nc, wv_words, Wv_words, c)
+
+        for b in range(BATCH):
+            x = k_sum[b]
+            squares = work.tile([P, KV_HEADS, 2, HALF], F32)
+            sum_sq = work.tile([P, KV_HEADS], F32)
+            for h in range(KV_HEADS):
+                nc.scalar.activation(
+                    out=squares[:, h], in_=x[:, h], func=ACT.Square, accum_out=sum_sq[:, h : h + 1]
+                )
+            by_cos = work.tile([P, KV_HEADS, 2, HALF], F32)
+            by_sin = work.tile([P, KV_HEADS, 2, HALF], F32)
+            all_heads = [P, KV_HEADS, 2, HALF]
+            nc.vector.tensor_tensor(
+                out=by_cos[:], in0=x[:], in1=cos_gain[:].unsqueeze(1).to_broadcast(all_heads), op=ALU.mult
+            )
+            nc.vector.tensor_tensor(
+                out=by_sin[:], in0=x[:], in1=sin_gain[:].unsqueeze(1).to_broadcast(all_heads), op=ALU.mult
+            )
+            rotated = work.tile([P, KV_HEADS, 2, HALF], F32)
+            for s in range(2):
+                nc.vector.tensor_tensor(
+                    out=rotated[:, :, s, :], in0=by_cos[:, :, s, :], in1=by_sin[:, :, 1 - s, :], op=ALU.add
+                )
+            mean_sq = work.tile([P, KV_HEADS], F32)
+            nc.vector.tensor_scalar(
+                out=mean_sq[:], in0=sum_sq[:], scalar1=1.0 / HEAD_DIM, scalar2=EPS, op0=ALU.mult, op1=ALU.add
+            )
+            rms = work.tile([P, KV_HEADS], F32)
+            nc.scalar.activation(out=rms[:], in_=mean_sq[:], func=ACT.Sqrt)
+            rstd = work.tile([P, KV_HEADS], F32)
+            nc.vector.reciprocal(out=rstd[:], in_=rms[:])
+            keys = work.tile([P, KV_HEADS, HEAD_DIM], F32)
+            nc.vector.tensor_tensor(
+                out=keys[:],
+                in0=rotated[:].rearrange("p h s c -> p h (s c)"),
+                in1=rstd[:].unsqueeze(2).to_broadcast([P, KV_HEADS, HEAD_DIM]),
+                op=ALU.mult,
+            )
+            store_heads(nc, out_0, b, keys[:])
+
+        for c in range(CHUNKS):
+            project(nc, v_sum, x_codes, x_planes, wv_words, wv_planes, c)
+        for b in range(BATCH):
+            values = work.tile([P, KV_HEADS, HEAD_DIM], F32)
+            source = v_sum[b][:].rearrange("p h s c -> p h (s c)")
+            if b % 2 == 0:
+                nc.vector.tensor_copy(out=values[:], in_=source)
+            else:
+                nc.scalar.copy(out=values[:], in_=source)
+            store_heads(nc, out_1, b, values[:])

@@ -38,9 +38,9 @@ FLOPS = 2 * BATCH * TOKENS * D_MODEL * 2 * N_COLS
 
 def load_scale_rows(nc, planes, scales):
     for r in range(SCALE_ROWS):
-        nc.sync.dma_start(
-            out=planes[r:P:32, :, :].bitcast(I32),
-            in_=scales[:, r : 4 * SCALE_ROWS : SCALE_ROWS, :].rearrange("g q n -> q g n").bitcast(I32),
+        nc.gpsimd.dma_start(
+            out=planes[r:P:32, :, :].bitcast(F32),
+            in_=scales[:, r : 4 * SCALE_ROWS : SCALE_ROWS, :].rearrange("g q n -> q g n").bitcast(F32),
         )
 
 
@@ -108,6 +108,9 @@ def tile_multiheadattention_pb_k_kernel(
         nc.scalar.dma_start(out=cos_sb[:], in_=cos)
         nc.scalar.dma_start(out=sin_sb[:], in_=sin)
 
+        load_scale_rows(nc, wk_planes, Wk_scales)
+        load_scale_rows(nc, wv_planes, Wv_scales)
+
         raw = {}
 
         def load_tokens(c):
@@ -115,10 +118,7 @@ def tile_multiheadattention_pb_k_kernel(
             columns = slice(c * CHUNK * K_PASS, (c + 1) * CHUNK * K_PASS)
             nc.sync.dma_start(out=raw[c][:], in_=kv_input[:, :, columns].rearrange("b t k -> t b k"))
 
-        load_tokens(0)
-        load_scale_rows(nc, wk_planes, Wk_scales)
-        load_weight_words(nc, wk_words, Wk_words, 0)
-        for c in range(1, PREFETCH):
+        for c in range(PREFETCH):
             load_tokens(c)
             load_weight_words(nc, wk_words, Wk_words, c)
 
@@ -176,7 +176,6 @@ def tile_multiheadattention_pb_k_kernel(
                 project(nc, k_sum, x_codes, x_planes, wk_words, wk_planes, c - 1)
         project(nc, k_sum, x_codes, x_planes, wk_words, wk_planes, CHUNKS - 1)
 
-        load_scale_rows(nc, wv_planes, Wv_scales)
         for c in range(CHUNKS):
             load_weight_words(nc, wv_words, Wv_words, c)
 

@@ -30,17 +30,18 @@ PASSES = D_MODEL // K_PASS
 CHUNK = 4
 CHUNKS = PASSES // CHUNK
 PAIRS = K_PASS // 2
-PREFETCH = 4
+PREFETCH = 3
 SCALE_ROWS = 4
+SORT_AHEAD = 2
 
 FLOPS = 2 * BATCH * TOKENS * D_MODEL * 2 * N_COLS
 
 
 def load_scale_rows(nc, planes, scales):
     for r in range(SCALE_ROWS):
-        nc.gpsimd.dma_start(
-            out=planes[r:P:32, :, :].bitcast(F32),
-            in_=scales[:, r : 4 * SCALE_ROWS : SCALE_ROWS, :].rearrange("g q n -> q g n").bitcast(F32),
+        nc.sync.dma_start(
+            out=planes[r:P:32, :, :].bitcast(I32),
+            in_=scales[:, r : 4 * SCALE_ROWS : SCALE_ROWS, :].rearrange("g q n -> q g n").bitcast(I32),
         )
 
 
@@ -79,6 +80,7 @@ def tile_multiheadattention_pb_k_kernel(
     with ExitStack() as ctx:
         keep = ctx.enter_context(tc.tile_pool(name="keep", bufs=1))
         raw_pool = ctx.enter_context(tc.tile_pool(name="raw", bufs=PREFETCH))
+        sorted_pool = ctx.enter_context(tc.tile_pool(name="sorted", bufs=SORT_AHEAD + 1))
         grouped_pool = ctx.enter_context(tc.tile_pool(name="grouped", bufs=2))
         work = ctx.enter_context(tc.tile_pool(name="work", bufs=2))
         banks = ctx.enter_context(tc.psum_pool(name="banks", bufs=4))
@@ -108,9 +110,6 @@ def tile_multiheadattention_pb_k_kernel(
         nc.scalar.dma_start(out=cos_sb[:], in_=cos)
         nc.scalar.dma_start(out=sin_sb[:], in_=sin)
 
-        load_scale_rows(nc, wk_planes, Wk_scales)
-        load_scale_rows(nc, wv_planes, Wv_scales)
-
         raw = {}
 
         def load_tokens(c):
@@ -118,7 +117,10 @@ def tile_multiheadattention_pb_k_kernel(
             columns = slice(c * CHUNK * K_PASS, (c + 1) * CHUNK * K_PASS)
             nc.sync.dma_start(out=raw[c][:], in_=kv_input[:, :, columns].rearrange("b t k -> t b k"))
 
-        for c in range(PREFETCH):
+        load_tokens(0)
+        load_scale_rows(nc, wk_planes, Wk_scales)
+        load_weight_words(nc, wk_words, Wk_words, 0)
+        for c in range(1, PREFETCH):
             load_tokens(c)
             load_weight_words(nc, wk_words, Wk_words, c)
 
@@ -138,23 +140,31 @@ def tile_multiheadattention_pb_k_kernel(
         )
         nc.vector.tensor_scalar_mul(out=sin_gain[:, 1, :], in0=sin_gain[:, 1, :], scalar1=-1.0)
 
-        def quantise_chunk(c):
+        by_parity = {}
+
+        def sort_chunk(c):
             pairs = raw[c][:].bitcast(F32)
+            by_parity[c] = sorted_pool.tile([P, CHUNK, BATCH, 2, P], F32, name="by_parity")
+            for j in range(CHUNK):
+                nc.scalar.copy(
+                    out=by_parity[c][:, j],
+                    in_=pairs[:, :, j * PAIRS : (j + 1) * PAIRS].rearrange("p b (i u) -> p b u i", u=2),
+                )
+            if c + PREFETCH < CHUNKS:
+                load_tokens(c + PREFETCH)
+                load_weight_words(nc, wk_words, Wk_words, c + PREFETCH)
+
+        def quantise_chunk(c):
             grouped = grouped_pool.tile([P, CHUNK * BATCH, TOKENS, PACK], BF16, align_bytes=64)
             grouped_pairs = grouped[:].bitcast(F32)
             for j in range(CHUNK):
                 bank = banks.tile([P, BATCH, 2, TOKENS], F32, tag="bank")
                 for b in range(BATCH):
                     for u in range(2):
-                        nc.tensor.transpose(
-                            bank[:, b, u, :], pairs[:, b, j * PAIRS + u : (j + 1) * PAIRS : 2], identity[:]
-                        )
+                        nc.tensor.transpose(bank[:, b, u, :], by_parity[c][:, j, b, u, :], identity[:])
                 target = grouped_pairs[:, j * BATCH : (j + 1) * BATCH, :, :]
                 source = bank[:].rearrange("p b u m -> p b m u")
-                if j % 2 == 0:
-                    nc.vector.tensor_copy(out=target, in_=source)
-                else:
-                    nc.scalar.copy(out=target, in_=source)
+                nc.vector.tensor_copy(out=target, in_=source)
             for half in range(2):
                 first = c * CHUNK + half * (CHUNK // 2)
                 passes = slice(first, first + CHUNK // 2)
@@ -167,15 +177,17 @@ def tile_multiheadattention_pb_k_kernel(
 
         k_sum = [sums.tile([P, KV_HEADS, 2, HALF], F32, name="k_sum%d" % b) for b in range(BATCH)]
         v_sum = [sums.tile([P, KV_HEADS, 2, HALF], F32, name="v_sum%d" % b) for b in range(BATCH)]
+        for c in range(SORT_AHEAD):
+            sort_chunk(c)
         for c in range(CHUNKS):
             quantise_chunk(c)
-            if c + PREFETCH < CHUNKS:
-                load_tokens(c + PREFETCH)
-                load_weight_words(nc, wk_words, Wk_words, c + PREFETCH)
+            if c + SORT_AHEAD < CHUNKS:
+                sort_chunk(c + SORT_AHEAD)
             if c > 0:
                 project(nc, k_sum, x_codes, x_planes, wk_words, wk_planes, c - 1)
         project(nc, k_sum, x_codes, x_planes, wk_words, wk_planes, CHUNKS - 1)
 
+        load_scale_rows(nc, wv_planes, Wv_scales)
         for c in range(CHUNKS):
             load_weight_words(nc, wv_words, Wv_words, c)
 

@@ -53,8 +53,8 @@ def load_weight_words(nc, words_sb, words, c):
     )
 
 
-def project(nc, acc, x_codes, x_planes, words_sb, planes, c):
-    for b in range(BATCH):
+def project(nc, acc, x_codes, x_planes, words_sb, planes, c, batches):
+    for b in batches:
         for g in range(c * CHUNK, (c + 1) * CHUNK):
             nc.tensor.matmul_mx(
                 out=acc[b][:].rearrange("p h s c -> p (h s c)"),
@@ -95,8 +95,6 @@ def tile_multiheadattention_pb_k_kernel(
         x_planes = keep.tile([P, PASSES, BATCH, TOKENS], U8, align_bytes=64)
 
         nc.vector.memset(wk_planes[:].bitcast(I32), 0)
-        nc.vector.memset(wv_planes[:].bitcast(I32), 0)
-
         identity = keep.tile([P, P], F32)
         make_identity(nc, identity[:])
 
@@ -104,6 +102,7 @@ def tile_multiheadattention_pb_k_kernel(
         ones = keep.tile([P, P], BF16)
         nc.gpsimd.memset(gain_row[:], 0.0)
         nc.gpsimd.memset(ones[:], 1.0)
+        nc.gpsimd.memset(wv_planes[:].bitcast(I32), 0)
         nc.scalar.dma_start(out=gain_row[0:1, :], in_=k_scale.unsqueeze(0))
         cos_sb = keep.tile([P, HALF], BF16)
         sin_sb = keep.tile([P, HALF], BF16)
@@ -114,8 +113,14 @@ def tile_multiheadattention_pb_k_kernel(
 
         def load_tokens(c):
             raw[c] = raw_pool.tile([P, BATCH, CHUNK * K_PASS], BF16, name="raw")
-            columns = slice(c * CHUNK * K_PASS, (c + 1) * CHUNK * K_PASS)
-            nc.sync.dma_start(out=raw[c][:], in_=kv_input[:, :, columns].rearrange("b t k -> t b k"))
+            pieces = 2 if c == 0 else 1
+            width = CHUNK * K_PASS // pieces
+            for i in range(pieces):
+                columns = slice(c * CHUNK * K_PASS + i * width, c * CHUNK * K_PASS + (i + 1) * width)
+                nc.sync.dma_start(
+                    out=raw[c][:, :, i * width : (i + 1) * width],
+                    in_=kv_input[:, :, columns].rearrange("b t k -> t b k"),
+                )
 
         load_tokens(0)
         load_scale_rows(nc, wk_planes, Wk_scales)
@@ -124,21 +129,23 @@ def tile_multiheadattention_pb_k_kernel(
             load_tokens(c)
             load_weight_words(nc, wk_words, Wk_words, c)
 
-        gain_bank = banks.tile([P, 2, HALF], F32, tag="bank")
-        nc.tensor.matmul(
-            out=gain_bank[:].rearrange("p s c -> p (s c)"), lhsT=ones[:], rhs=gain_row[:], start=True, stop=True
-        )
         gain = keep.tile([P, 2, HALF], F32)
         cos_gain = keep.tile([P, 2, HALF], F32)
         sin_gain = keep.tile([P, 2, HALF], F32)
-        nc.vector.tensor_scalar_add(out=gain[:], in0=gain_bank[:], scalar1=1.0)
-        nc.vector.tensor_tensor(
-            out=cos_gain[:], in0=gain[:], in1=cos_sb[:].unsqueeze(1).to_broadcast([P, 2, HALF]), op=ALU.mult
-        )
-        nc.vector.tensor_tensor(
-            out=sin_gain[:], in0=gain[:], in1=sin_sb[:].unsqueeze(1).to_broadcast([P, 2, HALF]), op=ALU.mult
-        )
-        nc.vector.tensor_scalar_mul(out=sin_gain[:, 1, :], in0=sin_gain[:, 1, :], scalar1=-1.0)
+
+        def rope_tables():
+            gain_bank = banks.tile([P, 2, HALF], F32, tag="bank")
+            nc.tensor.matmul(
+                out=gain_bank[:].rearrange("p s c -> p (s c)"), lhsT=ones[:], rhs=gain_row[:], start=True, stop=True
+            )
+            nc.vector.tensor_scalar_add(out=gain[:], in0=gain_bank[:], scalar1=1.0)
+            nc.vector.tensor_tensor(
+                out=cos_gain[:], in0=gain[:], in1=cos_sb[:].unsqueeze(1).to_broadcast([P, 2, HALF]), op=ALU.mult
+            )
+            nc.vector.tensor_tensor(
+                out=sin_gain[:], in0=gain[:], in1=sin_sb[:].unsqueeze(1).to_broadcast([P, 2, HALF]), op=ALU.mult
+            )
+            nc.vector.tensor_scalar_mul(out=sin_gain[:, 1, :], in0=sin_gain[:, 1, :], scalar1=-1.0)
 
         by_parity = {}
 
@@ -181,11 +188,13 @@ def tile_multiheadattention_pb_k_kernel(
             sort_chunk(c)
         for c in range(CHUNKS):
             quantise_chunk(c)
+            if c == 1:
+                rope_tables()
             if c + SORT_AHEAD < CHUNKS:
                 sort_chunk(c + SORT_AHEAD)
             if c > 0:
-                project(nc, k_sum, x_codes, x_planes, wk_words, wk_planes, c - 1)
-        project(nc, k_sum, x_codes, x_planes, wk_words, wk_planes, CHUNKS - 1)
+                project(nc, k_sum, x_codes, x_planes, wk_words, wk_planes, c - 1, range(BATCH))
+        project(nc, k_sum, x_codes, x_planes, wk_words, wk_planes, CHUNKS - 1, range(BATCH))
 
         load_scale_rows(nc, wv_planes, Wv_scales)
         for c in range(CHUNKS):
@@ -230,9 +239,9 @@ def tile_multiheadattention_pb_k_kernel(
             )
             store_heads(nc, out_0, b, keys[:])
 
-        for c in range(CHUNKS):
-            project(nc, v_sum, x_codes, x_planes, wv_words, wv_planes, c)
         for b in range(BATCH):
+            for c in range(CHUNKS):
+                project(nc, v_sum, x_codes, x_planes, wv_words, wv_planes, c, [b])
             values = work.tile([P, KV_HEADS, HEAD_DIM], F32)
             source = v_sum[b][:].rearrange("p h s c -> p h (s c)")
             if b % 2 == 0:

@@ -103,11 +103,8 @@ def tile_multiheadattention_pb_k_kernel(
         nc.gpsimd.memset(gain_row[:], 0.0)
         nc.gpsimd.memset(ones[:], 1.0)
         nc.gpsimd.memset(wv_planes[:].bitcast(I32), 0)
-        nc.scalar.dma_start(out=gain_row[0:1, :], in_=k_scale.unsqueeze(0))
         cos_sb = keep.tile([P, HALF], BF16)
         sin_sb = keep.tile([P, HALF], BF16)
-        nc.scalar.dma_start(out=cos_sb[:], in_=cos)
-        nc.scalar.dma_start(out=sin_sb[:], in_=sin)
 
         raw = {}
 
@@ -117,17 +114,18 @@ def tile_multiheadattention_pb_k_kernel(
             width = CHUNK * K_PASS // pieces
             for i in range(pieces):
                 columns = slice(c * CHUNK * K_PASS + i * width, c * CHUNK * K_PASS + (i + 1) * width)
-                nc.sync.dma_start(
+                nc.scalar.dma_start(
                     out=raw[c][:, :, i * width : (i + 1) * width],
                     in_=kv_input[:, :, columns].rearrange("b t k -> t b k"),
                 )
 
-        load_tokens(0)
         load_scale_rows(nc, wk_planes, Wk_scales)
-        load_weight_words(nc, wk_words, Wk_words, 0)
-        for c in range(1, PREFETCH):
+        for c in range(PREFETCH):
             load_tokens(c)
             load_weight_words(nc, wk_words, Wk_words, c)
+        nc.scalar.dma_start(out=gain_row[0:1, :], in_=k_scale.unsqueeze(0))
+        nc.scalar.dma_start(out=cos_sb[:], in_=cos)
+        nc.scalar.dma_start(out=sin_sb[:], in_=sin)
 
         gain = keep.tile([P, 2, HALF], F32)
         cos_gain = keep.tile([P, 2, HALF], F32)

@@ -70,7 +70,7 @@ def project(nc, acc, x_codes, x_planes, words_sb, planes, c, batches):
 def store_heads(nc, out, b, rows):
     by_repeat = out[b].rearrange("(h r) t d -> r t h d", r=REPEAT)
     for r in range(REPEAT):
-        nc.sync.dma_start(out=by_repeat[r], in_=rows)
+        nc.scalar.dma_start(out=by_repeat[r], in_=rows)
 
 
 def tile_multiheadattention_pb_k_kernel(
@@ -95,6 +95,8 @@ def tile_multiheadattention_pb_k_kernel(
         x_planes = keep.tile([P, PASSES, BATCH, TOKENS], U8, align_bytes=64)
 
         nc.vector.memset(wk_planes[:].bitcast(I32), 0)
+        warm = keep.tile([P, 1], F32)
+        nc.gpsimd.memset(warm[:], 0.0)
         identity = keep.tile([P, P], F32)
         make_identity(nc, identity[:])
 
@@ -102,9 +104,12 @@ def tile_multiheadattention_pb_k_kernel(
         ones = keep.tile([P, P], BF16)
         nc.gpsimd.memset(gain_row[:], 0.0)
         nc.gpsimd.memset(ones[:], 1.0)
-        nc.gpsimd.memset(wv_planes[:].bitcast(I32), 0)
         cos_sb = keep.tile([P, HALF], BF16)
         sin_sb = keep.tile([P, HALF], BF16)
+        nc.gpsimd.dma_start(out=gain_row[0:1, :], in_=k_scale.unsqueeze(0))
+        nc.gpsimd.dma_start(out=cos_sb[:], in_=cos)
+        nc.gpsimd.dma_start(out=sin_sb[:], in_=sin)
+        nc.gpsimd.memset(wv_planes[:].bitcast(I32), 0)
 
         raw = {}
 
@@ -119,13 +124,13 @@ def tile_multiheadattention_pb_k_kernel(
                     in_=kv_input[:, :, columns].rearrange("b t k -> t b k"),
                 )
 
+        load_tokens(0)
+        load_weight_words(nc, wk_words, Wk_words, 0)
         load_scale_rows(nc, wk_planes, Wk_scales)
-        for c in range(PREFETCH):
+        for c in range(1, PREFETCH):
             load_tokens(c)
             load_weight_words(nc, wk_words, Wk_words, c)
-        nc.scalar.dma_start(out=gain_row[0:1, :], in_=k_scale.unsqueeze(0))
-        nc.scalar.dma_start(out=cos_sb[:], in_=cos)
-        nc.scalar.dma_start(out=sin_sb[:], in_=sin)
+        nc.scalar.copy(out=warm[:], in_=warm[:])
 
         gain = keep.tile([P, 2, HALF], F32)
         cos_gain = keep.tile([P, 2, HALF], F32)
@@ -198,14 +203,18 @@ def tile_multiheadattention_pb_k_kernel(
         for c in range(CHUNKS):
             load_weight_words(nc, wv_words, Wv_words, c)
 
+        sums_sq, key_rows = [], []
         for b in range(BATCH):
-            x = k_sum[b]
             squares = work.tile([P, KV_HEADS, 2, HALF], F32)
             sum_sq = work.tile([P, KV_HEADS], F32)
             for h in range(KV_HEADS):
                 nc.scalar.activation(
-                    out=squares[:, h], in_=x[:, h], func=ACT.Square, accum_out=sum_sq[:, h : h + 1]
+                    out=squares[:, h], in_=k_sum[b][:, h], func=ACT.Square, accum_out=sum_sq[:, h : h + 1]
                 )
+            sums_sq.append(sum_sq)
+        for b in range(BATCH):
+            x = k_sum[b]
+            sum_sq = sums_sq[b]
             by_cos = work.tile([P, KV_HEADS, 2, HALF], F32)
             by_sin = work.tile([P, KV_HEADS, 2, HALF], F32)
             all_heads = [P, KV_HEADS, 2, HALF]
@@ -235,15 +244,14 @@ def tile_multiheadattention_pb_k_kernel(
                 in1=rstd[:].unsqueeze(2).to_broadcast([P, KV_HEADS, HEAD_DIM]),
                 op=ALU.mult,
             )
-            store_heads(nc, out_0, b, keys[:])
+            key_rows.append(keys)
+        for b in range(BATCH):
+            store_heads(nc, out_0, b, key_rows[b][:])
 
         for b in range(BATCH):
             for c in range(CHUNKS):
                 project(nc, v_sum, x_codes, x_planes, wv_words, wv_planes, c, [b])
             values = work.tile([P, KV_HEADS, HEAD_DIM], F32)
             source = v_sum[b][:].rearrange("p h s c -> p h (s c)")
-            if b % 2 == 0:
-                nc.vector.tensor_copy(out=values[:], in_=source)
-            else:
-                nc.scalar.copy(out=values[:], in_=source)
+            nc.vector.tensor_copy(out=values[:], in_=source)
             store_heads(nc, out_1, b, values[:])

@@ -32,17 +32,20 @@ CHUNKS = PASSES // CHUNK
 PAIRS = K_PASS // 2
 PREFETCH = 3
 SCALE_ROWS = 4
+SCALE_PASSES = 8
 SORT_AHEAD = 2
 
 FLOPS = 2 * BATCH * TOKENS * D_MODEL * 2 * N_COLS
 
 
 def load_scale_rows(nc, planes, scales):
-    for r in range(SCALE_ROWS):
-        nc.sync.dma_start(
-            out=planes[r:P:32, :, :].bitcast(I32),
-            in_=scales[:, r : 4 * SCALE_ROWS : SCALE_ROWS, :].rearrange("g q n -> q g n").bitcast(I32),
-        )
+    for first in range(0, PASSES, SCALE_PASSES):
+        passes = slice(first, first + SCALE_PASSES)
+        for r in range(SCALE_ROWS):
+            nc.sync.dma_start(
+                out=planes[r:P:32, passes, :].bitcast(I32),
+                in_=scales[passes, r : 4 * SCALE_ROWS : SCALE_ROWS, :].rearrange("g q n -> q g n").bitcast(I32),
+            )
 
 
 def load_weight_words(nc, words_sb, words, c):
@@ -119,15 +122,17 @@ def tile_multiheadattention_pb_k_kernel(
             width = CHUNK * K_PASS // pieces
             for i in range(pieces):
                 columns = slice(c * CHUNK * K_PASS + i * width, c * CHUNK * K_PASS + (i + 1) * width)
-                nc.scalar.dma_start(
+                nc.sync.dma_start(
                     out=raw[c][:, :, i * width : (i + 1) * width],
                     in_=kv_input[:, :, columns].rearrange("b t k -> t b k"),
                 )
 
         load_tokens(0)
-        load_weight_words(nc, wk_words, Wk_words, 0)
+        load_tokens(1)
         load_scale_rows(nc, wk_planes, Wk_scales)
-        for c in range(1, PREFETCH):
+        load_weight_words(nc, wk_words, Wk_words, 0)
+        load_weight_words(nc, wk_words, Wk_words, 1)
+        for c in range(2, PREFETCH):
             load_tokens(c)
             load_weight_words(nc, wk_words, Wk_words, c)
         nc.scalar.copy(out=warm[:], in_=warm[:])

@@ -32,20 +32,19 @@ CHUNKS = PASSES // CHUNK
 PAIRS = K_PASS // 2
 PREFETCH = 3
 SCALE_ROWS = 4
-SCALE_PASSES = 8
+SCALE_GROUPS = ((0, 8), (8, 16), (16, PASSES))
 SORT_AHEAD = 2
 
 FLOPS = 2 * BATCH * TOKENS * D_MODEL * 2 * N_COLS
 
 
-def load_scale_rows(nc, planes, scales):
-    for first in range(0, PASSES, SCALE_PASSES):
-        passes = slice(first, first + SCALE_PASSES)
-        for r in range(SCALE_ROWS):
-            nc.sync.dma_start(
-                out=planes[r:P:32, passes, :].bitcast(I32),
-                in_=scales[passes, r : 4 * SCALE_ROWS : SCALE_ROWS, :].rearrange("g q n -> q g n").bitcast(I32),
-            )
+def load_scale_rows(nc, groups, scales, i):
+    passes = slice(*SCALE_GROUPS[i])
+    for r in range(SCALE_ROWS):
+        nc.sync.dma_start(
+            out=groups[i][r:P:32, :, :].bitcast(I32),
+            in_=scales[passes, r : 4 * SCALE_ROWS : SCALE_ROWS, :].rearrange("g q n -> q g n").bitcast(I32),
+        )
 
 
 def load_weight_words(nc, words_sb, words, c):
@@ -64,7 +63,7 @@ def project(nc, acc, x_codes, x_planes, words_sb, planes, c, batches):
                 lhsT=x_codes[:, g, b, :].bitcast(FP8X4),
                 lhsT_scale=x_planes[:, g, b, :],
                 rhs=words_sb[:, g, :].bitcast(FP4X4),
-                rhs_scale=planes[:, g, :],
+                rhs_scale=planes[g],
                 start=(g == 0),
                 stop=(g == PASSES - 1),
             )
@@ -73,7 +72,7 @@ def project(nc, acc, x_codes, x_planes, words_sb, planes, c, batches):
 def store_heads(nc, out, b, rows):
     by_repeat = out[b].rearrange("(h r) t d -> r t h d", r=REPEAT)
     for r in range(REPEAT):
-        nc.scalar.dma_start(out=by_repeat[r], in_=rows)
+        nc.sync.dma_start(out=by_repeat[r], in_=rows)
 
 
 def tile_multiheadattention_pb_k_kernel(
@@ -85,21 +84,27 @@ def tile_multiheadattention_pb_k_kernel(
         raw_pool = ctx.enter_context(tc.tile_pool(name="raw", bufs=PREFETCH))
         sorted_pool = ctx.enter_context(tc.tile_pool(name="sorted", bufs=SORT_AHEAD + 1))
         grouped_pool = ctx.enter_context(tc.tile_pool(name="grouped", bufs=2))
-        work = ctx.enter_context(tc.tile_pool(name="work", bufs=2))
+        work = ctx.enter_context(tc.tile_pool(name="work", bufs=1))
         banks = ctx.enter_context(tc.psum_pool(name="banks", bufs=4))
         sums = ctx.enter_context(tc.psum_pool(name="sums", bufs=1))
         ctx.enter_context(tc.manual_schedule())
 
         wk_words = keep.tile([P, PASSES, 2 * N_COLS], U8, align_bytes=64)
         wv_words = keep.tile([P, PASSES, 2 * N_COLS], U8, align_bytes=64)
-        wk_planes = keep.tile([P, PASSES, N_COLS], U8, align_bytes=64)
-        wv_planes = keep.tile([P, PASSES, N_COLS], U8, align_bytes=64)
+        k_groups, v_groups, k_planes, v_planes = [], [], [], []
+        for groups, planes, name in ((k_groups, k_planes, "k"), (v_groups, v_planes, "v")):
+            for first, last in SCALE_GROUPS:
+                group = keep.tile([P, last - first, N_COLS], U8, name="%s_planes%d" % (name, first), align_bytes=64)
+                groups.append(group)
+                planes += [group[:, g, :] for g in range(last - first)]
         x_codes = keep.tile([P, PASSES, BATCH, TOKENS], U32, align_bytes=64)
         x_planes = keep.tile([P, PASSES, BATCH, TOKENS], U8, align_bytes=64)
 
-        nc.vector.memset(wk_planes[:].bitcast(I32), 0)
+        for group in k_groups:
+            nc.vector.memset(group[:].bitcast(I32), 0)
         warm = keep.tile([P, 1], F32)
         nc.gpsimd.memset(warm[:], 0.0)
+        nc.scalar.copy(out=warm[:], in_=warm[:])
         identity = keep.tile([P, P], F32)
         make_identity(nc, identity[:])
 
@@ -112,30 +117,34 @@ def tile_multiheadattention_pb_k_kernel(
         nc.gpsimd.dma_start(out=gain_row[0:1, :], in_=k_scale.unsqueeze(0))
         nc.gpsimd.dma_start(out=cos_sb[:], in_=cos)
         nc.gpsimd.dma_start(out=sin_sb[:], in_=sin)
-        nc.gpsimd.memset(wv_planes[:].bitcast(I32), 0)
+        for group in v_groups:
+            nc.gpsimd.memset(group[:].bitcast(I32), 0)
 
         raw = {}
 
         def load_tokens(c):
-            raw[c] = raw_pool.tile([P, BATCH, CHUNK * K_PASS], BF16, name="raw")
             pieces = 2 if c == 0 else 1
-            width = CHUNK * K_PASS // pieces
+            width = CHUNK // pieces
+            raw[c] = []
             for i in range(pieces):
-                columns = slice(c * CHUNK * K_PASS + i * width, c * CHUNK * K_PASS + (i + 1) * width)
+                if c == 0:
+                    tokens = keep.tile([P, BATCH, width * K_PASS], BF16, name="raw_first%d" % i)
+                else:
+                    tokens = raw_pool.tile([P, BATCH, width * K_PASS], BF16, name="raw")
+                start = (c * CHUNK + i * width) * K_PASS
                 nc.sync.dma_start(
-                    out=raw[c][:, :, i * width : (i + 1) * width],
-                    in_=kv_input[:, :, columns].rearrange("b t k -> t b k"),
+                    out=tokens[:], in_=kv_input[:, :, start : start + width * K_PASS].rearrange("b t k -> t b k")
                 )
+                pairs = tokens[:].bitcast(F32)
+                raw[c] += [pairs[:, :, j * PAIRS : (j + 1) * PAIRS] for j in range(width)]
 
         load_tokens(0)
-        load_tokens(1)
-        load_scale_rows(nc, wk_planes, Wk_scales)
+        load_scale_rows(nc, k_groups, Wk_scales, 0)
         load_weight_words(nc, wk_words, Wk_words, 0)
-        load_weight_words(nc, wk_words, Wk_words, 1)
-        for c in range(2, PREFETCH):
+        for c in range(1, PREFETCH):
             load_tokens(c)
             load_weight_words(nc, wk_words, Wk_words, c)
-        nc.scalar.copy(out=warm[:], in_=warm[:])
+        load_scale_rows(nc, k_groups, Wk_scales, 1)
 
         gain = keep.tile([P, 2, HALF], F32)
         cos_gain = keep.tile([P, 2, HALF], F32)
@@ -158,16 +167,17 @@ def tile_multiheadattention_pb_k_kernel(
         by_parity = {}
 
         def sort_chunk(c):
-            pairs = raw[c][:].bitcast(F32)
             by_parity[c] = sorted_pool.tile([P, CHUNK, BATCH, 2, P], F32, name="by_parity")
             for j in range(CHUNK):
                 nc.scalar.copy(
                     out=by_parity[c][:, j],
-                    in_=pairs[:, :, j * PAIRS : (j + 1) * PAIRS].rearrange("p b (i u) -> p b u i", u=2),
+                    in_=raw[c][j].rearrange("p b (i u) -> p b u i", u=2),
                 )
             if c + PREFETCH < CHUNKS:
                 load_tokens(c + PREFETCH)
                 load_weight_words(nc, wk_words, Wk_words, c + PREFETCH)
+            if c == 1:
+                load_scale_rows(nc, k_groups, Wk_scales, 2)
 
         def quantise_chunk(c):
             grouped = grouped_pool.tile([P, CHUNK * BATCH, TOKENS, PACK], BF16, align_bytes=64)
@@ -191,27 +201,28 @@ def tile_multiheadattention_pb_k_kernel(
                 )
 
         k_sum = [sums.tile([P, KV_HEADS, 2, HALF], F32, name="k_sum%d" % b) for b in range(BATCH)]
-        v_sum = [sums.tile([P, KV_HEADS, 2, HALF], F32, name="v_sum%d" % b) for b in range(BATCH)]
+        v_sum = sums.tile([P, KV_HEADS, 2, HALF], F32)
         for c in range(SORT_AHEAD):
             sort_chunk(c)
         for c in range(CHUNKS):
             quantise_chunk(c)
-            if c == 1:
+            if c == CHUNKS // 2:
                 rope_tables()
             if c + SORT_AHEAD < CHUNKS:
                 sort_chunk(c + SORT_AHEAD)
             if c > 0:
-                project(nc, k_sum, x_codes, x_planes, wk_words, wk_planes, c - 1, range(BATCH))
-        project(nc, k_sum, x_codes, x_planes, wk_words, wk_planes, CHUNKS - 1, range(BATCH))
+                project(nc, k_sum, x_codes, x_planes, wk_words, k_planes, c - 1, range(BATCH))
+        project(nc, k_sum, x_codes, x_planes, wk_words, k_planes, CHUNKS - 1, range(BATCH))
 
-        load_scale_rows(nc, wv_planes, Wv_scales)
-        for c in range(CHUNKS):
-            load_weight_words(nc, wv_words, Wv_words, c)
+        for i, (first, last) in enumerate(SCALE_GROUPS):
+            load_scale_rows(nc, v_groups, Wv_scales, i)
+            for c in range(first // CHUNK, last // CHUNK):
+                load_weight_words(nc, wv_words, Wv_words, c)
 
         sums_sq, key_rows = [], []
         for b in range(BATCH):
             squares = work.tile([P, KV_HEADS, 2, HALF], F32)
-            sum_sq = work.tile([P, KV_HEADS], F32)
+            sum_sq = keep.tile([P, KV_HEADS], F32, name="sum_sq%d" % b)
             for h in range(KV_HEADS):
                 nc.scalar.activation(
                     out=squares[:, h], in_=k_sum[b][:, h], func=ACT.Square, accum_out=sum_sq[:, h : h + 1]
@@ -242,7 +253,7 @@ def tile_multiheadattention_pb_k_kernel(
             nc.scalar.activation(out=rms[:], in_=mean_sq[:], func=ACT.Sqrt)
             rstd = work.tile([P, KV_HEADS], F32)
             nc.vector.reciprocal(out=rstd[:], in_=rms[:])
-            keys = work.tile([P, KV_HEADS, HEAD_DIM], F32)
+            keys = keep.tile([P, KV_HEADS, HEAD_DIM], F32, name="keys%d" % b)
             nc.vector.tensor_tensor(
                 out=keys[:],
                 in0=rotated[:].rearrange("p h s c -> p h (s c)"),
@@ -253,10 +264,27 @@ def tile_multiheadattention_pb_k_kernel(
         for b in range(BATCH):
             store_heads(nc, out_0, b, key_rows[b][:])
 
-        for b in range(BATCH):
-            for c in range(CHUNKS):
-                project(nc, v_sum, x_codes, x_planes, wv_words, wv_planes, c, [b])
-            values = work.tile([P, KV_HEADS, HEAD_DIM], F32)
-            source = v_sum[b][:].rearrange("p h s c -> p h (s c)")
-            nc.vector.tensor_copy(out=values[:], in_=source)
-            store_heads(nc, out_1, b, values[:])
+        for c in range(CHUNKS):
+            project(nc, [v_sum], x_codes, x_planes, wv_words, v_planes, c, [0])
+        values = keep.tile([P, KV_HEADS, HEAD_DIM], F32)
+        nc.vector.tensor_copy(out=values[:], in_=v_sum[:].rearrange("p h s c -> p h (s c)"))
+        store_heads(nc, out_1, 0, values[:])
+        last = BATCH - 1
+        for h in range(KV_HEADS):
+            head_sum = banks.tile([P, HEAD_DIM], F32, tag="bank")
+            for g in range(PASSES):
+                nc.tensor.matmul_mx(
+                    out=head_sum[:],
+                    lhsT=x_codes[:, g, last, :].bitcast(FP8X4),
+                    lhsT_scale=x_planes[:, g, last, :],
+                    rhs=wv_words[:, g, 2 * h * HEAD_DIM : 2 * (h + 1) * HEAD_DIM].bitcast(FP4X4),
+                    rhs_scale=v_planes[g][:, h * HEAD_DIM : (h + 1) * HEAD_DIM],
+                    start=(g == 0),
+                    stop=(g == PASSES - 1),
+                )
+            head_rows = keep.tile([P, HEAD_DIM], F32, name="head_rows%d" % h)
+            nc.vector.tensor_copy(out=head_rows[:], in_=head_sum[:])
+            nc.sync.dma_start(
+                out=out_1[last, h * REPEAT : (h + 1) * REPEAT].rearrange("r t d -> t r d"),
+                in_=head_rows[:].unsqueeze(1).to_broadcast([P, REPEAT, HEAD_DIM]),
+            )

@@ -32,27 +32,26 @@ CHUNKS = PASSES // CHUNK
 PAIRS = K_PASS // 2
 PREFETCH = 3
 SCALE_ROWS = 4
-SCALE_GROUPS = ((0, 8), (8, 16), (16, PASSES))
+GROUP = 2
+GROUP_PASSES = GROUP * CHUNK
 SORT_AHEAD = 2
 
 FLOPS = 2 * BATCH * TOKENS * D_MODEL * 2 * N_COLS
 
 
-def load_scale_rows(nc, groups, scales, i):
-    passes = slice(*SCALE_GROUPS[i])
-    for r in range(SCALE_ROWS):
-        nc.sync.dma_start(
-            out=groups[i][r:P:32, :, :].bitcast(I32),
-            in_=scales[passes, r : 4 * SCALE_ROWS : SCALE_ROWS, :].rearrange("g q n -> q g n").bitcast(I32),
-        )
-
-
-def load_weight_words(nc, words_sb, words, c):
+def load_weight_chunk(nc, words_sb, words, groups, scales, c):
     passes = slice(c * CHUNK, (c + 1) * CHUNK)
     nc.sync.dma_start(
         out=words_sb[:, passes, :].bitcast(I32),
         in_=words[passes].rearrange("g p n -> p g n").bitcast(I32),
     )
+    if c % GROUP == 0:
+        rows = scales[c * CHUNK : c * CHUNK + GROUP_PASSES]
+        for r in range(SCALE_ROWS):
+            nc.sync.dma_start(
+                out=groups[c // GROUP][r:P:32, :, :].bitcast(I32),
+                in_=rows[:, r : 4 * SCALE_ROWS : SCALE_ROWS, :].rearrange("g q n -> q g n").bitcast(I32),
+            )
 
 
 def project(nc, acc, x_codes, x_planes, words_sb, planes, c, batches):
@@ -93,10 +92,10 @@ def tile_multiheadattention_pb_k_kernel(
         wv_words = keep.tile([P, PASSES, 2 * N_COLS], U8, align_bytes=64)
         k_groups, v_groups, k_planes, v_planes = [], [], [], []
         for groups, planes, name in ((k_groups, k_planes, "k"), (v_groups, v_planes, "v")):
-            for first, last in SCALE_GROUPS:
-                group = keep.tile([P, last - first, N_COLS], U8, name="%s_planes%d" % (name, first), align_bytes=64)
+            for i in range(CHUNKS // GROUP):
+                group = keep.tile([P, GROUP_PASSES, N_COLS], U8, name="%s_planes%d" % (name, i), align_bytes=64)
                 groups.append(group)
-                planes += [group[:, g, :] for g in range(last - first)]
+                planes += [group[:, g, :] for g in range(GROUP_PASSES)]
         x_codes = keep.tile([P, PASSES, BATCH, TOKENS], U32, align_bytes=64)
         x_planes = keep.tile([P, PASSES, BATCH, TOKENS], U8, align_bytes=64)
 
@@ -138,13 +137,9 @@ def tile_multiheadattention_pb_k_kernel(
                 pairs = tokens[:].bitcast(F32)
                 raw[c] += [pairs[:, :, j * PAIRS : (j + 1) * PAIRS] for j in range(width)]
 
-        load_tokens(0)
-        load_scale_rows(nc, k_groups, Wk_scales, 0)
-        load_weight_words(nc, wk_words, Wk_words, 0)
-        for c in range(1, PREFETCH):
+        for c in range(PREFETCH):
             load_tokens(c)
-            load_weight_words(nc, wk_words, Wk_words, c)
-        load_scale_rows(nc, k_groups, Wk_scales, 1)
+            load_weight_chunk(nc, wk_words, Wk_words, k_groups, Wk_scales, c)
 
         gain = keep.tile([P, 2, HALF], F32)
         cos_gain = keep.tile([P, 2, HALF], F32)
@@ -175,9 +170,7 @@ def tile_multiheadattention_pb_k_kernel(
                 )
             if c + PREFETCH < CHUNKS:
                 load_tokens(c + PREFETCH)
-                load_weight_words(nc, wk_words, Wk_words, c + PREFETCH)
-            if c == 1:
-                load_scale_rows(nc, k_groups, Wk_scales, 2)
+                load_weight_chunk(nc, wk_words, Wk_words, k_groups, Wk_scales, c + PREFETCH)
 
         def quantise_chunk(c):
             grouped = grouped_pool.tile([P, CHUNK * BATCH, TOKENS, PACK], BF16, align_bytes=64)
@@ -214,10 +207,8 @@ def tile_multiheadattention_pb_k_kernel(
                 project(nc, k_sum, x_codes, x_planes, wk_words, k_planes, c - 1, range(BATCH))
         project(nc, k_sum, x_codes, x_planes, wk_words, k_planes, CHUNKS - 1, range(BATCH))
 
-        for i, (first, last) in enumerate(SCALE_GROUPS):
-            load_scale_rows(nc, v_groups, Wv_scales, i)
-            for c in range(first // CHUNK, last // CHUNK):
-                load_weight_words(nc, wv_words, Wv_words, c)
+        for c in range(CHUNKS):
+            load_weight_chunk(nc, wv_words, Wv_words, v_groups, Wv_scales, c)
 
         sums_sq, key_rows = [], []
         for b in range(BATCH):
@@ -264,17 +255,12 @@ def tile_multiheadattention_pb_k_kernel(
         for b in range(BATCH):
             store_heads(nc, out_0, b, key_rows[b][:])
 
-        for c in range(CHUNKS):
-            project(nc, [v_sum], x_codes, x_planes, wv_words, v_planes, c, [0])
-        values = keep.tile([P, KV_HEADS, HEAD_DIM], F32)
-        nc.vector.tensor_copy(out=values[:], in_=v_sum[:].rearrange("p h s c -> p h (s c)"))
-        store_heads(nc, out_1, 0, values[:])
         last = BATCH - 1
-        for h in range(KV_HEADS):
-            head_sum = banks.tile([P, HEAD_DIM], F32, tag="bank")
-            for g in range(PASSES):
+
+        def project_head(bank, h, c):
+            for g in range(c * CHUNK, (c + 1) * CHUNK):
                 nc.tensor.matmul_mx(
-                    out=head_sum[:],
+                    out=bank[:],
                     lhsT=x_codes[:, g, last, :].bitcast(FP8X4),
                     lhsT_scale=x_planes[:, g, last, :],
                     rhs=wv_words[:, g, 2 * h * HEAD_DIM : 2 * (h + 1) * HEAD_DIM].bitcast(FP4X4),
@@ -282,9 +268,25 @@ def tile_multiheadattention_pb_k_kernel(
                     start=(g == 0),
                     stop=(g == PASSES - 1),
                 )
+
+        def store_head(bank, h):
             head_rows = keep.tile([P, HEAD_DIM], F32, name="head_rows%d" % h)
-            nc.vector.tensor_copy(out=head_rows[:], in_=head_sum[:])
+            nc.vector.tensor_copy(out=head_rows[:], in_=bank[:])
             nc.sync.dma_start(
                 out=out_1[last, h * REPEAT : (h + 1) * REPEAT].rearrange("r t d -> t r d"),
                 in_=head_rows[:].unsqueeze(1).to_broadcast([P, REPEAT, HEAD_DIM]),
             )
+
+        head_sum = banks.tile([P, HEAD_DIM], F32, tag="bank")
+        for c in range(CHUNKS):
+            project(nc, [v_sum], x_codes, x_planes, wv_words, v_planes, c, [0])
+            project_head(head_sum, 0, c)
+        values = keep.tile([P, KV_HEADS, HEAD_DIM], F32)
+        nc.vector.tensor_copy(out=values[:], in_=v_sum[:].rearrange("p h s c -> p h (s c)"))
+        store_heads(nc, out_1, 0, values[:])
+        store_head(head_sum, 0)
+        for h in range(1, KV_HEADS):
+            head_sum = banks.tile([P, HEAD_DIM], F32, tag="bank")
+            for c in range(CHUNKS):
+                project_head(head_sum, h, c)
+            store_head(head_sum, h)

from contextlib import ExitStack

import concourse.mybir as mybir
from concourse.masks import make_identity

F32 = mybir.dt.float32
BF16 = mybir.dt.bfloat16
I32 = mybir.dt.int32
U32 = mybir.dt.uint32
U8 = mybir.dt.uint8
FP8X4 = mybir.dt.float8_e4m3fn_x4
FP4X4 = mybir.dt.float4_e2m1fn_x4
ALU = mybir.AluOpType
ACT = mybir.ActivationFunctionType

P = 128
PACK = 4
K_PASS = P * PACK
BATCH = 2
TOKENS = 128
D_MODEL = 16384
KV_HEADS = 4
HEAD_DIM = 128
HALF = HEAD_DIM // 2
REPEAT = 4
N_COLS = KV_HEADS * HEAD_DIM
EPS = 1e-6

PASSES = D_MODEL // K_PASS
CHUNK = 4
CHUNKS = PASSES // CHUNK
PAIRS = K_PASS // 2
PREFETCH = 3
SCALE_ROWS = 4
GROUP = 2
GROUP_PASSES = GROUP * CHUNK
SORT_AHEAD = 2

FLOPS = 2 * BATCH * TOKENS * D_MODEL * 2 * N_COLS


def load_weight_chunk(nc, words_sb, words, groups, scales, c):
    passes = slice(c * CHUNK, (c + 1) * CHUNK)
    nc.sync.dma_start(
        out=words_sb[:, passes, :].bitcast(I32),
        in_=words[passes].rearrange("g p n -> p g n").bitcast(I32),
    )
    if c % GROUP == 0:
        rows = scales[c * CHUNK : c * CHUNK + GROUP_PASSES]
        for r in range(SCALE_ROWS):
            nc.sync.dma_start(
                out=groups[c // GROUP][r:P:32, :, :].bitcast(I32),
                in_=rows[:, r : 4 * SCALE_ROWS : SCALE_ROWS, :].rearrange("g q n -> q g n").bitcast(I32),
            )


def project(nc, acc, x_codes, x_planes, words_sb, planes, c, batches):
    for b in batches:
        for g in range(c * CHUNK, (c + 1) * CHUNK):
            nc.tensor.matmul_mx(
                out=acc[b][:].rearrange("p h s c -> p (h s c)"),
                lhsT=x_codes[:, g, b, :].bitcast(FP8X4),
                lhsT_scale=x_planes[:, g, b, :],
                rhs=words_sb[:, g, :].bitcast(FP4X4),
                rhs_scale=planes[g],
                start=(g == 0),
                stop=(g == PASSES - 1),
            )


def store_heads(nc, out, b, rows):
    by_repeat = out[b].rearrange("(h r) t d -> r t h d", r=REPEAT)
    for r in range(REPEAT):
        nc.sync.dma_start(out=by_repeat[r], in_=rows)


def tile_multiheadattention_pb_k_kernel(
    tc, kv_input, Wk_words, Wk_scales, Wv_words, Wv_scales, k_scale, cos, sin, out_0, out_1
):
    nc = tc.nc
    with ExitStack() as ctx:
        keep = ctx.enter_context(tc.tile_pool(name="keep", bufs=1))
        raw_pool = ctx.enter_context(tc.tile_pool(name="raw", bufs=PREFETCH))
        sorted_pool = ctx.enter_context(tc.tile_pool(name="sorted", bufs=SORT_AHEAD + 1))
        grouped_pool = ctx.enter_context(tc.tile_pool(name="grouped", bufs=2))
        work = ctx.enter_context(tc.tile_pool(name="work", bufs=1))
        banks = ctx.enter_context(tc.psum_pool(name="banks", bufs=4))
        sums = ctx.enter_context(tc.psum_pool(name="sums", bufs=1))
        ctx.enter_context(tc.manual_schedule())

        wk_words = keep.tile([P, PASSES, 2 * N_COLS], U8, align_bytes=64)
        wv_words = keep.tile([P, PASSES, 2 * N_COLS], U8, align_bytes=64)
        k_groups, v_groups, k_planes, v_planes = [], [], [], []
        for groups, planes, name in ((k_groups, k_planes, "k"), (v_groups, v_planes, "v")):
            for i in range(CHUNKS // GROUP):
                group = keep.tile([P, GROUP_PASSES, N_COLS], U8, name="%s_planes%d" % (name, i), align_bytes=64)
                groups.append(group)
                planes += [group[:, g, :] for g in range(GROUP_PASSES)]
        x_codes = keep.tile([P, PASSES, BATCH, TOKENS], U32, align_bytes=64)
        x_planes = keep.tile([P, PASSES, BATCH, TOKENS], U8, align_bytes=64)

        for group in k_groups:
            nc.vector.memset(group[:].bitcast(I32), 0)
        warm = keep.tile([P, 1], F32)
        nc.gpsimd.memset(warm[:], 0.0)
        nc.scalar.copy(out=warm[:], in_=warm[:])
        identity = keep.tile([P, P], F32)
        make_identity(nc, identity[:])

        gain_row = keep.tile([P, HEAD_DIM], BF16)
        ones = keep.tile([P, P], BF16)
        nc.gpsimd.memset(gain_row[:], 0.0)
        nc.gpsimd.memset(ones[:], 1.0)
        cos_sb = keep.tile([P, HALF], BF16)
        sin_sb = keep.tile([P, HALF], BF16)
        nc.gpsimd.dma_start(out=gain_row[0:1, :], in_=k_scale.unsqueeze(0))
        nc.gpsimd.dma_start(out=cos_sb[:], in_=cos)
        nc.gpsimd.dma_start(out=sin_sb[:], in_=sin)
        for group in v_groups:
            nc.gpsimd.memset(group[:].bitcast(I32), 0)

        raw = {}

        def load_tokens(c):
            pieces = 2 if c == 0 else 1
            width = CHUNK // pieces
            raw[c] = []
            for i in range(pieces):
                if c == 0:
                    tokens = keep.tile([P, BATCH, width * K_PASS], BF16, name="raw_first%d" % i)
                else:
                    tokens = raw_pool.tile([P, BATCH, width * K_PASS], BF16, name="raw")
                start = (c * CHUNK + i * width) * K_PASS
                nc.sync.dma_start(
                    out=tokens[:], in_=kv_input[:, :, start : start + width * K_PASS].rearrange("b t k -> t b k")
                )
                pairs = tokens[:].bitcast(F32)
                raw[c] += [pairs[:, :, j * PAIRS : (j + 1) * PAIRS] for j in range(width)]

        for c in range(PREFETCH):
            load_tokens(c)
            load_weight_chunk(nc, wk_words, Wk_words, k_groups, Wk_scales, c)

        gain = keep.tile([P, 2, HALF], F32)
        cos_gain = keep.tile([P, 2, HALF], F32)
        sin_gain = keep.tile([P, 2, HALF], F32)

        def rope_tables():
            gain_bank = banks.tile([P, 2, HALF], F32, tag="bank")
            nc.tensor.matmul(
                out=gain_bank[:].rearrange("p s c -> p (s c)"), lhsT=ones[:], rhs=gain_row[:], start=True, stop=True
            )
            nc.vector.tensor_scalar_add(out=gain[:], in0=gain_bank[:], scalar1=1.0)
            nc.vector.tensor_tensor(
                out=cos_gain[:], in0=gain[:], in1=cos_sb[:].unsqueeze(1).to_broadcast([P, 2, HALF]), op=ALU.mult
            )
            nc.vector.tensor_tensor(
                out=sin_gain[:], in0=gain[:], in1=sin_sb[:].unsqueeze(1).to_broadcast([P, 2, HALF]), op=ALU.mult
            )
            nc.vector.tensor_scalar_mul(out=sin_gain[:, 1, :], in0=sin_gain[:, 1, :], scalar1=-1.0)

        by_parity = {}

        def sort_chunk(c):
            by_parity[c] = sorted_pool.tile([P, CHUNK, BATCH, 2, P], F32, name="by_parity")
            for j in range(CHUNK):
                nc.scalar.copy(
                    out=by_parity[c][:, j],
                    in_=raw[c][j].rearrange("p b (i u) -> p b u i", u=2),
                )
            if c + PREFETCH < CHUNKS:
                load_tokens(c + PREFETCH)
                load_weight_chunk(nc, wk_words, Wk_words, k_groups, Wk_scales, c + PREFETCH)

        def quantise_chunk(c):
            grouped = grouped_pool.tile([P, CHUNK * BATCH, TOKENS, PACK], BF16, align_bytes=64)
            grouped_pairs = grouped[:].bitcast(F32)
            for j in range(CHUNK):
                bank = banks.tile([P, BATCH, 2, TOKENS], F32, tag="bank")
                for b in range(BATCH):
                    for u in range(2):
                        nc.tensor.transpose(bank[:, b, u, :], by_parity[c][:, j, b, u, :], identity[:])
                target = grouped_pairs[:, j * BATCH : (j + 1) * BATCH, :, :]
                source = bank[:].rearrange("p b u m -> p b m u")
                nc.vector.tensor_copy(out=target, in_=source)
            for half in range(2):
                first = c * CHUNK + half * (CHUNK // 2)
                passes = slice(first, first + CHUNK // 2)
                units = slice(half * (CHUNK // 2) * BATCH, (half + 1) * (CHUNK // 2) * BATCH)
                nc.vector.quantize_mx(
                    out=x_codes[:, passes, :, :].rearrange("p g b m -> p (g b m)").bitcast(FP8X4),
                    scales=x_planes[:, passes, :, :].rearrange("p g b m -> p (g b m)"),
                    in_=grouped[:, units, :, :].rearrange("p a m t -> p (a m t)"),
                )

        k_sum = [sums.tile([P, KV_HEADS, 2, HALF], F32, name="k_sum%d" % b) for b in range(BATCH)]
        v_sum = sums.tile([P, KV_HEADS, 2, HALF], F32)
        for c in range(SORT_AHEAD):
            sort_chunk(c)
        for c in range(CHUNKS):
            quantise_chunk(c)
            if c == CHUNKS // 2:
                rope_tables()
            if c + SORT_AHEAD < CHUNKS:
                sort_chunk(c + SORT_AHEAD)
            if c > 0:
                project(nc, k_sum, x_codes, x_planes, wk_words, k_planes, c - 1, range(BATCH))
        project(nc, k_sum, x_codes, x_planes, wk_words, k_planes, CHUNKS - 1, range(BATCH))

        for c in range(CHUNKS):
            load_weight_chunk(nc, wv_words, Wv_words, v_groups, Wv_scales, c)

        sums_sq, key_rows = [], []
        for b in range(BATCH):
            squares = work.tile([P, KV_HEADS, 2, HALF], F32)
            sum_sq = keep.tile([P, KV_HEADS], F32, name="sum_sq%d" % b)
            for h in range(KV_HEADS):
                nc.scalar.activation(
                    out=squares[:, h], in_=k_sum[b][:, h], func=ACT.Square, accum_out=sum_sq[:, h : h + 1]
                )
            sums_sq.append(sum_sq)
        for b in range(BATCH):
            x = k_sum[b]
            sum_sq = sums_sq[b]
            by_cos = work.tile([P, KV_HEADS, 2, HALF], F32)
            by_sin = work.tile([P, KV_HEADS, 2, HALF], F32)
            all_heads = [P, KV_HEADS, 2, HALF]
            nc.vector.tensor_tensor(
                out=by_cos[:], in0=x[:], in1=cos_gain[:].unsqueeze(1).to_broadcast(all_heads), op=ALU.mult
            )
            nc.vector.tensor_tensor(
                out=by_sin[:], in0=x[:], in1=sin_gain[:].unsqueeze(1).to_broadcast(all_heads), op=ALU.mult
            )
            rotated = work.tile([P, KV_HEADS, 2, HALF], F32)
            for s in range(2):
                nc.vector.tensor_tensor(
                    out=rotated[:, :, s, :], in0=by_cos[:, :, s, :], in1=by_sin[:, :, 1 - s, :], op=ALU.add
                )
            mean_sq = work.tile([P, KV_HEADS], F32)
            nc.vector.tensor_scalar(
                out=mean_sq[:], in0=sum_sq[:], scalar1=1.0 / HEAD_DIM, scalar2=EPS, op0=ALU.mult, op1=ALU.add
            )
            rms = work.tile([P, KV_HEADS], F32)
            nc.scalar.activation(out=rms[:], in_=mean_sq[:], func=ACT.Sqrt)
            rstd = work.tile([P, KV_HEADS], F32)
            nc.vector.reciprocal(out=rstd[:], in_=rms[:])
            keys = keep.tile([P, KV_HEADS, HEAD_DIM], F32, name="keys%d" % b)
            nc.vector.tensor_tensor(
                out=keys[:],
                in0=rotated[:].rearrange("p h s c -> p h (s c)"),
                in1=rstd[:].unsqueeze(2).to_broadcast([P, KV_HEADS, HEAD_DIM]),
                op=ALU.mult,
            )
            key_rows.append(keys)
        for b in range(BATCH):
            store_heads(nc, out_0, b, key_rows[b][:])

        last = BATCH - 1

        def project_head(bank, h, c):
            for g in range(c * CHUNK, (c + 1) * CHUNK):
                nc.tensor.matmul_mx(
                    out=bank[:],
                    lhsT=x_codes[:, g, last, :].bitcast(FP8X4),
                    lhsT_scale=x_planes[:, g, last, :],
                    rhs=wv_words[:, g, 2 * h * HEAD_DIM : 2 * (h + 1) * HEAD_DIM].bitcast(FP4X4),
                    rhs_scale=v_planes[g][:, h * HEAD_DIM : (h + 1) * HEAD_DIM],
                    start=(g == 0),
                    stop=(g == PASSES - 1),
                )

        def store_head(bank, h):
            head_rows = keep.tile([P, HEAD_DIM], F32, name="head_rows%d" % h)
            nc.vector.tensor_copy(out=head_rows[:], in_=bank[:])
            nc.sync.dma_start(
                out=out_1[last, h * REPEAT : (h + 1) * REPEAT].rearrange("r t d -> t r d"),
                in_=head_rows[:].unsqueeze(1).to_broadcast([P, REPEAT, HEAD_DIM]),
            )

        head_sum = banks.tile([P, HEAD_DIM], F32, tag="bank")
        for c in range(CHUNKS):
            project(nc, [v_sum], x_codes, x_planes, wv_words, v_planes, c, [0])
            project_head(head_sum, 0, c)
        values = keep.tile([P, KV_HEADS, HEAD_DIM], F32)
        nc.vector.tensor_copy(out=values[:], in_=v_sum[:].rearrange("p h s c -> p h (s c)"))
        store_heads(nc, out_1, 0, values[:])
        store_head(head_sum, 0)
        for h in range(1, KV_HEADS):
            head_sum = banks.tile([P, HEAD_DIM], F32, tag="bank")
            for c in range(CHUNKS):
                project_head(head_sum, h, c)
            store_head(head_sum, h)
